import numpy as np
import ml_dtypes


def mxq(x, axis, fmt="e4m3"):
    dtype, down = {"e4m3": (ml_dtypes.float8_e4m3fn, 7), "e5m2": (ml_dtypes.float8_e5m2, 14)}[fmt]
    v = np.moveaxis(np.asarray(x, np.float32).astype(ml_dtypes.bfloat16).astype(np.float64), axis, -1)
    blocks = v.reshape(v.shape[:-1] + (-1, 32))
    amax = np.abs(blocks).max(-1, keepdims=True)
    byte = np.maximum(np.where(amax > 0, np.frexp(amax)[1] - 1 + 127, 0) - down, 1)
    scale = np.exp2(byte - 127.0)
    codes = (blocks / scale).astype(np.float32).astype(dtype).astype(np.float64)
    return np.moveaxis((codes * scale).reshape(v.shape), -1, axis)


WIDE = False


def mx_kscale(k):
    if not WIDE:
        return np.ones(k)
    levels = np.array([10, -10, 5, -5, 0])
    a = np.random.permutation(np.resize(levels, k // 512 * 4)).reshape(k // 512, 4)
    idx = np.arange(k)
    return np.exp2(a[idx // 512, idx % 128 // 32])


BF16 = ml_dtypes.bfloat16


def bf(x):
    return np.asarray(x, np.float32).astype(BF16)


def f64(x):
    return np.asarray(x).astype(np.float64)


B, S, Dm, H = 2, 64, 512, 16
D = Dm // H
ROPE_BASE = 10000.0


def _rope(t):
    theta = 1.0 / (ROPE_BASE ** (np.arange(0, D, 2, dtype=np.float64) / D))
    pos = np.arange(H, dtype=np.float64)[:, None]
    ang = pos * theta
    sin, cos = np.sin(ang), np.cos(ang)
    te, to = t[..., 0::2], t[..., 1::2]
    re = te * cos - to * sin
    ro = te * sin + to * cos
    return np.stack([re, ro], axis=-1).reshape(B, S, H, D)


def setup_inputs():
    s = mx_kscale(Dm)
    sc = 1.0 / np.sqrt(Dm)
    return {"x": bf(np.random.standard_normal((B, S, Dm)) * s),
            "Wq": bf(np.random.standard_normal((Dm, Dm)) * sc / s[:, None]),
            "Wk": bf(np.random.standard_normal((Dm, Dm)) * sc / s[:, None]),
            "Wv": bf(np.random.standard_normal((Dm, Dm)) * sc / s[:, None]),
            "st_pos": 0}


def reference(x, Wq, Wk, Wv, st_pos):
    xq = mxq(f64(x), 2, "e4m3")
    q = (xq @ mxq(f64(Wq), 0, "e4m3")).reshape(B, S, H, D)
    k = (xq @ mxq(f64(Wk), 0, "e4m3")).reshape(B, S, H, D)
    v = (xq @ mxq(f64(Wv), 0, "e4m3")).reshape(B, S, H, D)
    q = _rope(q)
    k = _rope(k)
    return q, k, v

@@ -1,0 +1,174 @@
+import math
+
+import concourse.masks as masks
+import concourse.mybir as mybir
+
+F32 = mybir.dt.float32
+BF16 = mybir.dt.bfloat16
+I32 = mybir.dt.int32
+U32 = mybir.dt.uint32
+U8 = mybir.dt.uint8
+FP8X4 = mybir.dt.float8_e4m3fn_x4
+ALU = mybir.AluOpType
+ACT = mybir.ActivationFunctionType
+
+P = 128
+PACK = 4
+K = P * PACK
+N = 512
+HEADS = 16
+HEAD_DIM = N // HEADS
+FREQS = HEAD_DIM // 2
+PAIRS = HEADS * FREQS
+ROPE_BASE = 10000.0
+ROUND_TO_INTEGER = 1.5 * 2.0**23
+
+VECTOR_COLUMNS = 256
+
+FLOPS = 3 * 2 * P * K * N
+
+
+def build_rotation_table(nc, pool):
+    head_index = pool.tile([P, HEADS, 1], I32)
+    nc.gpsimd.iota(out=head_index[:], pattern=[[1, HEADS], [0, 1]], base=0, channel_multiplier=0)
+
+    turns = pool.tile([P, HEADS, FREQS], F32)
+    nc.vector.tensor_scalar(
+        out=turns[:, :, 0:1],
+        in0=head_index[:],
+        scalar1=1.0 / (2.0 * math.pi),
+        scalar2=None,
+        op0=ALU.mult,
+    )
+    done = 1
+    while done < FREQS:
+        nc.vector.tensor_scalar(
+            out=turns[:, :, done : 2 * done],
+            in0=turns[:, :, 0:done],
+            scalar1=ROPE_BASE ** (-float(done) / FREQS),
+            scalar2=None,
+            op0=ALU.mult,
+        )
+        done *= 2
+    turns_flat = turns[:].rearrange("p h i -> p (h i)")
+
+    whole_turns = pool.tile([P, PAIRS], F32)
+    nc.vector.tensor_scalar(
+        out=whole_turns[:],
+        in0=turns_flat,
+        scalar1=ROUND_TO_INTEGER,
+        scalar2=ROUND_TO_INTEGER,
+        op0=ALU.add,
+        op1=ALU.subtract,
+    )
+    phase = pool.tile([P, 3, PAIRS], F32)
+    minus_abs = pool.tile([P, PAIRS], F32)
+    nc.vector.tensor_tensor(out=phase[:, 0, :], in0=whole_turns[:], in1=turns_flat, op=ALU.subtract)
+    nc.vector.tensor_tensor(out=phase[:, 2, :], in0=turns_flat, in1=whole_turns[:], op=ALU.subtract)
+    nc.vector.tensor_tensor(out=minus_abs[:], in0=phase[:, 0, :], in1=phase[:, 2, :], op=ALU.min)
+    nc.vector.tensor_scalar(
+        out=phase[:, 1, :], in0=minus_abs[:], scalar1=0.25, scalar2=None, op0=ALU.add
+    )
+    table = pool.tile([P, 3, PAIRS], F32)
+    nc.scalar.activation(out=table[:], in_=phase[:], func=ACT.Sin, scale=2.0 * math.pi)
+    return table
+
+
+def quantise_tokens(nc, pool, psum, x):
+    x_rows = pool.tile([P, K], BF16)
+    nc.sync.dma_start(out=x_rows[:], in_=x.rearrange("b s k -> (b s) k"))
+
+    identity = pool.tile([P, P], F32)
+    masks.make_identity(nc, identity[:])
+
+    x_words = x_rows[:].bitcast(F32).rearrange("r (p u) -> r u p", u=2)
+    x_flipped = psum.tile([P, 2, P], F32)
+    for u in range(2):
+        nc.tensor.transpose(x_flipped[:, u, :], x_words[:, u, :], identity[:])
+
+    x_grouped = pool.tile([P, P * PACK], BF16, align_bytes=64)
+    nc.scalar.copy(
+        out=x_grouped[:].bitcast(F32).rearrange("p (r u) -> p r u", u=2),
+        in_=x_flipped[:].rearrange("p u r -> p r u"),
+    )
+    x_codes = pool.tile([P, P], U32, align_bytes=64)
+    x_scales = pool.tile([P, P], U8, align_bytes=64)
+    nc.vector.quantize_mx(out=x_codes[:].bitcast(FP8X4), scales=x_scales[:], in_=x_grouped[:])
+    return x_codes, x_scales
+
+
+def regroup(copy, w_grouped, w_rows, columns):
+    copy(
+        out=w_grouped[:, columns, :].rearrange("p (c i) t -> p c t i", i=4),
+        in_=w_rows[:, :, columns].rearrange("p t (c i) -> p c t i", i=4),
+    )
+
+
+def rotate(nc, pool, product, table, name):
+    pairs = product[:].rearrange("p (c e) -> p c e", e=2)
+    cos_sin = table[:, 1:3, :].rearrange("p e c -> p c e")
+    minus_sin_cos = table[:, 0:2, :].rearrange("p e c -> p c e")
+    from_even = pool.tile([P, PAIRS, 2], F32, name=name + "_from_even")
+    from_odd = pool.tile([P, PAIRS, 2], F32, name=name + "_from_odd")
+    nc.vector.tensor_tensor(
+        out=from_even[:], in0=pairs[:, :, 0:1].to_broadcast([P, PAIRS, 2]), in1=cos_sin, op=ALU.mult
+    )
+    nc.vector.tensor_tensor(
+        out=from_odd[:],
+        in0=pairs[:, :, 1:2].to_broadcast([P, PAIRS, 2]),
+        in1=minus_sin_cos,
+        op=ALU.mult,
+    )
+    nc.vector.tensor_tensor(out=from_even[:], in0=from_even[:], in1=from_odd[:], op=ALU.add)
+    return from_even
+
+
+def tile_selfattention_s_kernel(tc, x, Wq, Wk, Wv, st_pos, out_0, out_1, out_2):
+    nc = tc.nc
+    with tc.tile_pool(name="sbuf", bufs=1) as pool, tc.psum_pool(name="psum", bufs=1) as psum:
+        zero = pool.tile([P, 1], F32)
+        unused = pool.tile([P, 1], F32)
+        nc.vector.memset(zero[:], 0.0)
+        nc.scalar.activation(out=unused[:], in_=zero[:], func=ACT.Sin)
+
+        x_codes, x_scales = quantise_tokens(nc, pool, psum, x)
+
+        projections = (("q", Wq, out_0), ("k", Wk, out_1), ("v", Wv, out_2))
+        rows_of = {}
+        for name, weight, out in projections:
+            w_rows = pool.tile([P, PACK, N], BF16, name=name + "_rows")
+            nc.sync.dma_start(out=w_rows[:], in_=weight.rearrange("(p t) n -> p t n", t=PACK))
+            rows_of[name] = w_rows
+
+        table = build_rotation_table(nc, pool)
+
+        for name, weight, out in projections:
+            w_grouped = pool.tile([P, N, PACK], BF16, name=name + "_grouped", align_bytes=64)
+            regroup(nc.vector.tensor_copy, w_grouped, rows_of[name], slice(0, VECTOR_COLUMNS))
+            regroup(nc.scalar.copy, w_grouped, rows_of[name], slice(VECTOR_COLUMNS, N))
+            w_codes = pool.tile([P, N], U32, name=name + "_codes", align_bytes=64)
+            w_scales = pool.tile([P, N], U8, name=name + "_scales", align_bytes=64)
+            nc.vector.quantize_mx(
+                out=w_codes[:].bitcast(FP8X4),
+                scales=w_scales[:],
+                in_=w_grouped[:].rearrange("p n t -> p (n t)"),
+            )
+            product = psum.tile([P, N], F32, name=name + "_product")
+            nc.tensor.matmul_mx(
+                out=product[:],
+                lhsT=x_codes[:].bitcast(FP8X4),
+                lhsT_scale=x_scales[:],
+                rhs=w_codes[:].bitcast(FP8X4),
+                rhs_scale=w_scales[:],
+                start=True,
+                stop=True,
+            )
+            if name == "v":
+                result = pool.tile([P, PAIRS, 2], F32, name="v_result")
+                nc.scalar.copy(out=result[:].rearrange("p c e -> p (c e)"), in_=product[:])
+            else:
+                result = rotate(nc, pool, product, table, name)
+            nc.sync.dma_start(
+                out=out.rearrange("b s h d -> (b s) (h d)"),
+                in_=result[:].rearrange("p c e -> p (c e)"),
+            )

@@ -23,12 +23,12 @@ PAIRS = HEADS * FREQS
 ROPE_BASE = 10000.0
 ROUND_TO_INTEGER = 1.5 * 2.0**23
 
-VECTOR_COLUMNS = 256
+VECTOR_COLUMNS = 344
 
 FLOPS = 3 * 2 * P * K * N
 
 
-def build_rotation_table(nc, pool):
+def build_rotation_phases(nc, pool):
     head_index = pool.tile([P, HEADS, 1], I32)
     nc.gpsimd.iota(out=head_index[:], pattern=[[1, HEADS], [0, 1]], base=0, channel_multiplier=0)
 
@@ -69,15 +69,10 @@ def build_rotation_table(nc, pool):
     nc.vector.tensor_scalar(
         out=phase[:, 1, :], in0=minus_abs[:], scalar1=0.25, scalar2=None, op0=ALU.add
     )
-    table = pool.tile([P, 3, PAIRS], F32)
-    nc.scalar.activation(out=table[:], in_=phase[:], func=ACT.Sin, scale=2.0 * math.pi)
-    return table
+    return phase
 
 
-def quantise_tokens(nc, pool, psum, x):
-    x_rows = pool.tile([P, K], BF16)
-    nc.sync.dma_start(out=x_rows[:], in_=x.rearrange("b s k -> (b s) k"))
-
+def quantise_tokens(nc, pool, psum, x_rows):
     identity = pool.tile([P, P], F32)
     masks.make_identity(nc, identity[:])
 
@@ -104,7 +99,28 @@ def regroup(copy, w_grouped, w_rows, columns):
     )
 
 
-def rotate(nc, pool, product, table, name):
+def quantise_and_multiply(nc, pool, psum, w_grouped, x_codes, x_scales, name):
+    w_codes = pool.tile([P, N], U32, name=name + "_codes", align_bytes=64)
+    w_scales = pool.tile([P, N], U8, name=name + "_scales", align_bytes=64)
+    nc.vector.quantize_mx(
+        out=w_codes[:].bitcast(FP8X4),
+        scales=w_scales[:],
+        in_=w_grouped[:].rearrange("p n t -> p (n t)"),
+    )
+    product = psum.tile([P, N], F32, name=name + "_product")
+    nc.tensor.matmul_mx(
+        out=product[:],
+        lhsT=x_codes[:].bitcast(FP8X4),
+        lhsT_scale=x_scales[:],
+        rhs=w_codes[:].bitcast(FP8X4),
+        rhs_scale=w_scales[:],
+        start=True,
+        stop=True,
+    )
+    return product
+
+
+def rotation_terms(nc, pool, product, table, name):
     pairs = product[:].rearrange("p (c e) -> p c e", e=2)
     cos_sin = table[:, 1:3, :].rearrange("p e c -> p c e")
     minus_sin_cos = table[:, 0:2, :].rearrange("p e c -> p c e")
@@ -119,56 +135,65 @@ def rotate(nc, pool, product, table, name):
         in1=minus_sin_cos,
         op=ALU.mult,
     )
+    return from_even, from_odd
+
+
+def add_and_store(nc, terms, out):
+    from_even, from_odd = terms
     nc.vector.tensor_tensor(out=from_even[:], in0=from_even[:], in1=from_odd[:], op=ALU.add)
-    return from_even
+    nc.sync.dma_start(
+        out=out.rearrange("b s h d -> (b s) (h d)"), in_=from_even[:].rearrange("p c e -> p (c e)")
+    )
 
 
 def tile_selfattention_s_kernel(tc, x, Wq, Wk, Wv, st_pos, out_0, out_1, out_2):
     nc = tc.nc
-    with tc.tile_pool(name="sbuf", bufs=1) as pool, tc.psum_pool(name="psum", bufs=1) as psum:
+    with (
+        tc.tile_pool(name="sbuf", bufs=1) as pool,
+        tc.psum_pool(name="psum", bufs=1) as psum,
+        tc.manual_schedule(),
+    ):
         zero = pool.tile([P, 1], F32)
         unused = pool.tile([P, 1], F32)
         nc.vector.memset(zero[:], 0.0)
         nc.scalar.activation(out=unused[:], in_=zero[:], func=ACT.Sin)
 
-        x_codes, x_scales = quantise_tokens(nc, pool, psum, x)
-
-        projections = (("q", Wq, out_0), ("k", Wk, out_1), ("v", Wv, out_2))
+        x_rows = pool.tile([P, K], BF16)
+        nc.sync.dma_start(out=x_rows[:], in_=x.rearrange("b s k -> (b s) k"))
         rows_of = {}
-        for name, weight, out in projections:
-            w_rows = pool.tile([P, PACK, N], BF16, name=name + "_rows")
-            nc.sync.dma_start(out=w_rows[:], in_=weight.rearrange("(p t) n -> p t n", t=PACK))
-            rows_of[name] = w_rows
-
-        table = build_rotation_table(nc, pool)
-
-        for name, weight, out in projections:
-            w_grouped = pool.tile([P, N, PACK], BF16, name=name + "_grouped", align_bytes=64)
-            regroup(nc.vector.tensor_copy, w_grouped, rows_of[name], slice(0, VECTOR_COLUMNS))
-            regroup(nc.scalar.copy, w_grouped, rows_of[name], slice(VECTOR_COLUMNS, N))
-            w_codes = pool.tile([P, N], U32, name=name + "_codes", align_bytes=64)
-            w_scales = pool.tile([P, N], U8, name=name + "_scales", align_bytes=64)
-            nc.vector.quantize_mx(
-                out=w_codes[:].bitcast(FP8X4),
-                scales=w_scales[:],
-                in_=w_grouped[:].rearrange("p n t -> p (n t)"),
-            )
-            product = psum.tile([P, N], F32, name=name + "_product")
-            nc.tensor.matmul_mx(
-                out=product[:],
-                lhsT=x_codes[:].bitcast(FP8X4),
-                lhsT_scale=x_scales[:],
-                rhs=w_codes[:].bitcast(FP8X4),
-                rhs_scale=w_scales[:],
-                start=True,
-                stop=True,
-            )
-            if name == "v":
-                result = pool.tile([P, PAIRS, 2], F32, name="v_result")
-                nc.scalar.copy(out=result[:].rearrange("p c e -> p (c e)"), in_=product[:])
-            else:
-                result = rotate(nc, pool, product, table, name)
+        grouped_of = {}
+        for name, weight in (("q", Wq), ("k", Wk), ("v", Wv)):
+            rows_of[name] = pool.tile([P, PACK, N], BF16, name=name + "_rows")
+            grouped_of[name] = pool.tile([P, N, PACK], BF16, name=name + "_grouped", align_bytes=64)
             nc.sync.dma_start(
-                out=out.rearrange("b s h d -> (b s) (h d)"),
-                in_=result[:].rearrange("p c e -> p (c e)"),
+                out=rows_of[name][:], in_=weight.rearrange("(p t) n -> p t n", t=PACK)
             )
+
+        phase = build_rotation_phases(nc, pool)
+        x_codes, x_scales = quantise_tokens(nc, pool, psum, x_rows)
+
+        vector_share = slice(0, VECTOR_COLUMNS)
+        scalar_share = slice(VECTOR_COLUMNS, N)
+
+        regroup(nc.vector.tensor_copy, grouped_of["q"], rows_of["q"], vector_share)
+        regroup(nc.scalar.copy, grouped_of["q"], rows_of["q"], scalar_share)
+        q_product = quantise_and_multiply(nc, pool, psum, grouped_of["q"], x_codes, x_scales, "q")
+
+        table = pool.tile([P, 3, PAIRS], F32)
+        nc.scalar.activation(out=table[:], in_=phase[:], func=ACT.Sin, scale=2.0 * math.pi)
+
+        regroup(nc.vector.tensor_copy, grouped_of["k"], rows_of["k"], vector_share)
+        regroup(nc.scalar.copy, grouped_of["k"], rows_of["k"], scalar_share)
+        regroup(nc.scalar.copy, grouped_of["v"], rows_of["v"], slice(0, N))
+
+        q_terms = rotation_terms(nc, pool, q_product, table, "q")
+        k_product = quantise_and_multiply(nc, pool, psum, grouped_of["k"], x_codes, x_scales, "k")
+        add_and_store(nc, q_terms, out_0)
+
+        v_product = quantise_and_multiply(nc, pool, psum, grouped_of["v"], x_codes, x_scales, "v")
+        v_result = pool.tile([P, N], F32)
+        nc.scalar.copy(out=v_result[:], in_=v_product[:])
+        nc.sync.dma_start(out=out_2.rearrange("b s h d -> (b s) (h d)"), in_=v_result[:])
+
+        k_terms = rotation_terms(nc, pool, k_product, table, "k")
+        add_and_store(nc, k_terms, out_1)

@@ -28,10 +28,7 @@ VECTOR_COLUMNS = 344
 FLOPS = 3 * 2 * P * K * N
 
 
-def build_rotation_phases(nc, pool):
-    head_index = pool.tile([P, HEADS, 1], I32)
-    nc.gpsimd.iota(out=head_index[:], pattern=[[1, HEADS], [0, 1]], base=0, channel_multiplier=0)
-
+def build_rotation_phases(nc, pool, head_index):
     turns = pool.tile([P, HEADS, FREQS], F32)
     nc.vector.tensor_scalar(
         out=turns[:, :, 0:1],
@@ -61,21 +58,20 @@ def build_rotation_phases(nc, pool):
         op0=ALU.add,
         op1=ALU.subtract,
     )
-    phase = pool.tile([P, 3, PAIRS], F32)
-    minus_abs = pool.tile([P, PAIRS], F32)
-    nc.vector.tensor_tensor(out=phase[:, 0, :], in0=whole_turns[:], in1=turns_flat, op=ALU.subtract)
-    nc.vector.tensor_tensor(out=phase[:, 2, :], in0=turns_flat, in1=whole_turns[:], op=ALU.subtract)
-    nc.vector.tensor_tensor(out=minus_abs[:], in0=phase[:, 0, :], in1=phase[:, 2, :], op=ALU.min)
-    nc.vector.tensor_scalar(
-        out=phase[:, 1, :], in0=minus_abs[:], scalar1=0.25, scalar2=None, op0=ALU.add
+    phase = pool.tile([P, 2, PAIRS], F32)
+    nc.vector.tensor_tensor(out=phase[:, 0, :], in0=turns_flat, in1=whole_turns[:], op=ALU.subtract)
+    nc.vector.scalar_tensor_tensor(
+        out=phase[:, 1, :],
+        in0=phase[:, 0, :],
+        scalar=-1.0,
+        in1=phase[:, 0, :],
+        op0=ALU.mult,
+        op1=ALU.min,
     )
     return phase
 
 
-def quantise_tokens(nc, pool, psum, x_rows):
-    identity = pool.tile([P, P], F32)
-    masks.make_identity(nc, identity[:])
-
+def quantise_tokens(nc, pool, psum, x_rows, identity):
     x_words = x_rows[:].bitcast(F32).rearrange("r (p u) -> r u p", u=2)
     x_flipped = psum.tile([P, 2, P], F32)
     for u in range(2):
@@ -138,9 +134,9 @@ def rotation_terms(nc, pool, product, table, name):
     return from_even, from_odd
 
 
-def add_and_store(nc, terms, out):
+def add_and_store(nc, add_engine, terms, out):
     from_even, from_odd = terms
-    nc.vector.tensor_tensor(out=from_even[:], in0=from_even[:], in1=from_odd[:], op=ALU.add)
+    add_engine.tensor_tensor(out=from_even[:], in0=from_even[:], in1=from_odd[:], op=ALU.add)
     nc.sync.dma_start(
         out=out.rearrange("b s h d -> (b s) (h d)"), in_=from_even[:].rearrange("p c e -> p (c e)")
     )
@@ -157,6 +153,10 @@ def tile_selfattention_s_kernel(tc, x, Wq, Wk, Wv, st_pos, out_0, out_1, out_2):
         unused = pool.tile([P, 1], F32)
         nc.vector.memset(zero[:], 0.0)
         nc.scalar.activation(out=unused[:], in_=zero[:], func=ACT.Sin)
+        quarter_turn = pool.tile([P, 1], F32)
+        nc.vector.tensor_scalar(
+            out=quarter_turn[:], in0=zero[:], scalar1=math.pi / 2.0, scalar2=None, op0=ALU.add
+        )
 
         x_rows = pool.tile([P, K], BF16)
         nc.sync.dma_start(out=x_rows[:], in_=x.rearrange("b s k -> (b s) k"))
@@ -169,8 +169,14 @@ def tile_selfattention_s_kernel(tc, x, Wq, Wk, Wv, st_pos, out_0, out_1, out_2):
                 out=rows_of[name][:], in_=weight.rearrange("(p t) n -> p t n", t=PACK)
             )
 
-        phase = build_rotation_phases(nc, pool)
-        x_codes, x_scales = quantise_tokens(nc, pool, psum, x_rows)
+        head_index = pool.tile([P, HEADS, 1], I32)
+        nc.gpsimd.iota(
+            out=head_index[:], pattern=[[1, HEADS], [0, 1]], base=0, channel_multiplier=0
+        )
+        identity = pool.tile([P, P], F32)
+        masks.make_identity(nc, identity[:])
+        phase = build_rotation_phases(nc, pool, head_index)
+        x_codes, x_scales = quantise_tokens(nc, pool, psum, x_rows, identity)
 
         vector_share = slice(0, VECTOR_COLUMNS)
         scalar_share = slice(VECTOR_COLUMNS, N)
@@ -180,15 +186,28 @@ def tile_selfattention_s_kernel(tc, x, Wq, Wk, Wv, st_pos, out_0, out_1, out_2):
         q_product = quantise_and_multiply(nc, pool, psum, grouped_of["q"], x_codes, x_scales, "q")
 
         table = pool.tile([P, 3, PAIRS], F32)
-        nc.scalar.activation(out=table[:], in_=phase[:], func=ACT.Sin, scale=2.0 * math.pi)
+        nc.scalar.activation(
+            out=table[:, 2, :], in_=phase[:, 0, :], func=ACT.Sin, scale=2.0 * math.pi
+        )
+        nc.scalar.activation(
+            out=table[:, 0, :], in_=phase[:, 0, :], func=ACT.Sin, scale=-2.0 * math.pi
+        )
 
         regroup(nc.vector.tensor_copy, grouped_of["k"], rows_of["k"], vector_share)
         regroup(nc.scalar.copy, grouped_of["k"], rows_of["k"], scalar_share)
+        nc.scalar.activation(
+            out=table[:, 1, :],
+            in_=phase[:, 1, :],
+            func=ACT.Sin,
+            scale=2.0 * math.pi,
+            bias=quarter_turn[:],
+        )
         regroup(nc.scalar.copy, grouped_of["v"], rows_of["v"], slice(0, N))
 
-        q_terms = rotation_terms(nc, pool, q_product, table, "q")
         k_product = quantise_and_multiply(nc, pool, psum, grouped_of["k"], x_codes, x_scales, "k")
-        add_and_store(nc, q_terms, out_0)
+
+        q_terms = rotation_terms(nc, pool, q_product, table, "q")
+        add_and_store(nc, nc.gpsimd, q_terms, out_0)
 
         v_product = quantise_and_multiply(nc, pool, psum, grouped_of["v"], x_codes, x_scales, "v")
         v_result = pool.tile([P, N], F32)
@@ -196,4 +215,4 @@ def tile_selfattention_s_kernel(tc, x, Wq, Wk, Wv, st_pos, out_0, out_1, out_2):
         nc.sync.dma_start(out=out_2.rearrange("b s h d -> (b s) (h d)"), in_=v_result[:])
 
         k_terms = rotation_terms(nc, pool, k_product, table, "k")
-        add_and_store(nc, k_terms, out_1)
+        add_and_store(nc, nc.vector, k_terms, out_1)

@@ -24,6 +24,7 @@ ROPE_BASE = 10000.0
 ROUND_TO_INTEGER = 1.5 * 2.0**23
 
 VECTOR_COLUMNS = 344
+VECTOR_COLUMNS_OF_WV = 128
 
 FLOPS = 3 * 2 * P * K * N
 
@@ -39,14 +40,15 @@ def build_rotation_phases(nc, pool, head_index):
     )
     done = 1
     while done < FREQS:
-        nc.vector.tensor_scalar(
-            out=turns[:, :, done : 2 * done],
-            in0=turns[:, :, 0:done],
-            scalar1=ROPE_BASE ** (-float(done) / FREQS),
-            scalar2=None,
-            op0=ALU.mult,
-        )
-        done *= 2
+        for shift in (done, 2 * done, 3 * done):
+            nc.vector.tensor_scalar(
+                out=turns[:, :, shift : shift + done],
+                in0=turns[:, :, 0:done],
+                scalar1=ROPE_BASE ** (-float(shift) / FREQS),
+                scalar2=None,
+                op0=ALU.mult,
+            )
+        done *= 4
     turns_flat = turns[:].rearrange("p h i -> p (h i)")
 
     whole_turns = pool.tile([P, PAIRS], F32)
@@ -71,7 +73,7 @@ def build_rotation_phases(nc, pool, head_index):
     return phase
 
 
-def quantise_tokens(nc, pool, psum, x_rows, identity):
+def group_tokens(nc, pool, psum, x_rows, identity):
     x_words = x_rows[:].bitcast(F32).rearrange("r (p u) -> r u p", u=2)
     x_flipped = psum.tile([P, 2, P], F32)
     for u in range(2):
@@ -82,10 +84,7 @@ def quantise_tokens(nc, pool, psum, x_rows, identity):
         out=x_grouped[:].bitcast(F32).rearrange("p (r u) -> p r u", u=2),
         in_=x_flipped[:].rearrange("p u r -> p r u"),
     )
-    x_codes = pool.tile([P, P], U32, align_bytes=64)
-    x_scales = pool.tile([P, P], U8, align_bytes=64)
-    nc.vector.quantize_mx(out=x_codes[:].bitcast(FP8X4), scales=x_scales[:], in_=x_grouped[:])
-    return x_codes, x_scales
+    return x_grouped
 
 
 def regroup(copy, w_grouped, w_rows, columns):
@@ -176,13 +175,16 @@ def tile_selfattention_s_kernel(tc, x, Wq, Wk, Wv, st_pos, out_0, out_1, out_2):
         identity = pool.tile([P, P], F32)
         masks.make_identity(nc, identity[:])
         phase = build_rotation_phases(nc, pool, head_index)
-        x_codes, x_scales = quantise_tokens(nc, pool, psum, x_rows, identity)
+        x_grouped = group_tokens(nc, pool, psum, x_rows, identity)
 
         vector_share = slice(0, VECTOR_COLUMNS)
         scalar_share = slice(VECTOR_COLUMNS, N)
 
         regroup(nc.vector.tensor_copy, grouped_of["q"], rows_of["q"], vector_share)
         regroup(nc.scalar.copy, grouped_of["q"], rows_of["q"], scalar_share)
+        x_codes = pool.tile([P, P], U32, align_bytes=64)
+        x_scales = pool.tile([P, P], U8, align_bytes=64)
+        nc.vector.quantize_mx(out=x_codes[:].bitcast(FP8X4), scales=x_scales[:], in_=x_grouped[:])
         q_product = quantise_and_multiply(nc, pool, psum, grouped_of["q"], x_codes, x_scales, "q")
 
         table = pool.tile([P, 3, PAIRS], F32)
@@ -202,7 +204,8 @@ def tile_selfattention_s_kernel(tc, x, Wq, Wk, Wv, st_pos, out_0, out_1, out_2):
             scale=2.0 * math.pi,
             bias=quarter_turn[:],
         )
-        regroup(nc.scalar.copy, grouped_of["v"], rows_of["v"], slice(0, N))
+        regroup(nc.vector.tensor_copy, grouped_of["v"], rows_of["v"], slice(0, VECTOR_COLUMNS_OF_WV))
+        regroup(nc.scalar.copy, grouped_of["v"], rows_of["v"], slice(VECTOR_COLUMNS_OF_WV, N))
 
         k_product = quantise_and_multiply(nc, pool, psum, grouped_of["k"], x_codes, x_scales, "k")
 

@@ -31,14 +31,15 @@ FLOPS = 3 * 2 * P * K * N
 
 def build_rotation_phases(nc, pool, head_index):
     turns = pool.tile([P, HEADS, FREQS], F32)
-    nc.vector.tensor_scalar(
-        out=turns[:, :, 0:1],
-        in0=head_index[:],
-        scalar1=1.0 / (2.0 * math.pi),
-        scalar2=None,
-        op0=ALU.mult,
-    )
-    done = 1
+    done = 4
+    for i in range(done):
+        nc.vector.tensor_scalar(
+            out=turns[:, :, i : i + 1],
+            in0=head_index[:],
+            scalar1=ROPE_BASE ** (-float(i) / FREQS) / (2.0 * math.pi),
+            scalar2=None,
+            op0=ALU.mult,
+        )
     while done < FREQS:
         for shift in (done, 2 * done, 3 * done):
             nc.vector.tensor_scalar(
@@ -62,6 +63,10 @@ def build_rotation_phases(nc, pool, head_index):
     )
     phase = pool.tile([P, 2, PAIRS], F32)
     nc.vector.tensor_tensor(out=phase[:, 0, :], in0=turns_flat, in1=whole_turns[:], op=ALU.subtract)
+    return phase
+
+
+def finish_rotation_phases(nc, phase):
     nc.vector.scalar_tensor_tensor(
         out=phase[:, 1, :],
         in0=phase[:, 0, :],
@@ -70,7 +75,6 @@ def build_rotation_phases(nc, pool, head_index):
         op0=ALU.mult,
         op1=ALU.min,
     )
-    return phase
 
 
 def group_tokens(nc, pool, psum, x_rows, identity):
@@ -94,7 +98,7 @@ def regroup(copy, w_grouped, w_rows, columns):
     )
 
 
-def quantise_and_multiply(nc, pool, psum, w_grouped, x_codes, x_scales, name):
+def quantise(nc, pool, w_grouped, name):
     w_codes = pool.tile([P, N], U32, name=name + "_codes", align_bytes=64)
     w_scales = pool.tile([P, N], U8, name=name + "_scales", align_bytes=64)
     nc.vector.quantize_mx(
@@ -102,6 +106,10 @@ def quantise_and_multiply(nc, pool, psum, w_grouped, x_codes, x_scales, name):
         scales=w_scales[:],
         in_=w_grouped[:].rearrange("p n t -> p (n t)"),
     )
+    return w_codes, w_scales
+
+
+def multiply(nc, psum, w_codes, w_scales, x_codes, x_scales, name):
     product = psum.tile([P, N], F32, name=name + "_product")
     nc.tensor.matmul_mx(
         out=product[:],
@@ -113,6 +121,11 @@ def quantise_and_multiply(nc, pool, psum, w_grouped, x_codes, x_scales, name):
         stop=True,
     )
     return product
+
+
+def quantise_and_multiply(nc, pool, psum, w_grouped, x_codes, x_scales, name):
+    w_codes, w_scales = quantise(nc, pool, w_grouped, name)
+    return multiply(nc, psum, w_codes, w_scales, x_codes, x_scales, name)
 
 
 def rotation_terms(nc, pool, product, table, name):
@@ -158,7 +171,6 @@ def tile_selfattention_s_kernel(tc, x, Wq, Wk, Wv, st_pos, out_0, out_1, out_2):
         )
 
         x_rows = pool.tile([P, K], BF16)
-        nc.sync.dma_start(out=x_rows[:], in_=x.rearrange("b s k -> (b s) k"))
         rows_of = {}
         grouped_of = {}
         for name, weight in (("q", Wq), ("k", Wk), ("v", Wv)):
@@ -167,6 +179,8 @@ def tile_selfattention_s_kernel(tc, x, Wq, Wk, Wv, st_pos, out_0, out_1, out_2):
             nc.sync.dma_start(
                 out=rows_of[name][:], in_=weight.rearrange("(p t) n -> p t n", t=PACK)
             )
+            if name == "q":
+                nc.sync.dma_start(out=x_rows[:], in_=x.rearrange("b s k -> (b s) k"))
 
         head_index = pool.tile([P, HEADS, 1], I32)
         nc.gpsimd.iota(
@@ -175,17 +189,19 @@ def tile_selfattention_s_kernel(tc, x, Wq, Wk, Wv, st_pos, out_0, out_1, out_2):
         identity = pool.tile([P, P], F32)
         masks.make_identity(nc, identity[:])
         phase = build_rotation_phases(nc, pool, head_index)
-        x_grouped = group_tokens(nc, pool, psum, x_rows, identity)
 
         vector_share = slice(0, VECTOR_COLUMNS)
         scalar_share = slice(VECTOR_COLUMNS, N)
 
         regroup(nc.vector.tensor_copy, grouped_of["q"], rows_of["q"], vector_share)
         regroup(nc.scalar.copy, grouped_of["q"], rows_of["q"], scalar_share)
+        x_grouped = group_tokens(nc, pool, psum, x_rows, identity)
+        finish_rotation_phases(nc, phase)
+        q_codes, q_scales = quantise(nc, pool, grouped_of["q"], "q")
         x_codes = pool.tile([P, P], U32, align_bytes=64)
         x_scales = pool.tile([P, P], U8, align_bytes=64)
         nc.vector.quantize_mx(out=x_codes[:].bitcast(FP8X4), scales=x_scales[:], in_=x_grouped[:])
-        q_product = quantise_and_multiply(nc, pool, psum, grouped_of["q"], x_codes, x_scales, "q")
+        q_product = multiply(nc, psum, q_codes, q_scales, x_codes, x_scales, "q")
 
         table = pool.tile([P, 3, PAIRS], F32)
         nc.scalar.activation(

@@ -23,63 +23,31 @@ PAIRS = HEADS * FREQS
 ROPE_BASE = 10000.0
 ROUND_TO_INTEGER = 1.5 * 2.0**23
 
-VECTOR_COLUMNS = 344
-VECTOR_COLUMNS_OF_WV = 128
+VECTOR_COLUMNS = 320
+VECTOR_COLUMNS_OF_WK = 256
+VECTOR_FIRST_COLUMNS_OF_WV = 64
+VECTOR_COLUMNS_OF_WV = 288
+SCALAR_FIRST_COLUMNS_OF_WV = 96
+
+BLOCKS = N // P
 
 FLOPS = 3 * 2 * P * K * N
 
 
-def build_rotation_phases(nc, pool, head_index):
-    turns = pool.tile([P, HEADS, FREQS], F32)
-    done = 4
-    for i in range(done):
-        nc.vector.tensor_scalar(
-            out=turns[:, :, i : i + 1],
-            in0=head_index[:],
-            scalar1=ROPE_BASE ** (-float(i) / FREQS) / (2.0 * math.pi),
-            scalar2=None,
-            op0=ALU.mult,
-        )
-    while done < FREQS:
-        for shift in (done, 2 * done, 3 * done):
-            nc.vector.tensor_scalar(
-                out=turns[:, :, shift : shift + done],
-                in0=turns[:, :, 0:done],
-                scalar1=ROPE_BASE ** (-float(shift) / FREQS),
-                scalar2=None,
-                op0=ALU.mult,
-            )
-        done *= 4
-    turns_flat = turns[:].rearrange("p h i -> p (h i)")
-
-    whole_turns = pool.tile([P, PAIRS], F32)
+def round_to_integer(nc, out, in_):
     nc.vector.tensor_scalar(
-        out=whole_turns[:],
-        in0=turns_flat,
+        out=out,
+        in0=in_,
         scalar1=ROUND_TO_INTEGER,
         scalar2=ROUND_TO_INTEGER,
         op0=ALU.add,
         op1=ALU.subtract,
     )
-    phase = pool.tile([P, 2, PAIRS], F32)
-    nc.vector.tensor_tensor(out=phase[:, 0, :], in0=turns_flat, in1=whole_turns[:], op=ALU.subtract)
-    return phase
-
-
-def finish_rotation_phases(nc, phase):
-    nc.vector.scalar_tensor_tensor(
-        out=phase[:, 1, :],
-        in0=phase[:, 0, :],
-        scalar=-1.0,
-        in1=phase[:, 0, :],
-        op0=ALU.mult,
-        op1=ALU.min,
-    )
 
 
 def group_tokens(nc, pool, psum, x_rows, identity):
     x_words = x_rows[:].bitcast(F32).rearrange("r (p u) -> r u p", u=2)
-    x_flipped = psum.tile([P, 2, P], F32)
+    x_flipped = psum.tile([P, 2, P], F32, tag="x_flipped")
     for u in range(2):
         nc.tensor.transpose(x_flipped[:, u, :], x_words[:, u, :], identity[:])
 
@@ -110,7 +78,7 @@ def quantise(nc, pool, w_grouped, name):
 
 
 def multiply(nc, psum, w_codes, w_scales, x_codes, x_scales, name):
-    product = psum.tile([P, N], F32, name=name + "_product")
+    product = psum.tile([P, N], F32, name=name + "_product", tag="x_flipped")
     nc.tensor.matmul_mx(
         out=product[:],
         lhsT=x_codes[:].bitcast(FP8X4),
@@ -123,35 +91,18 @@ def multiply(nc, psum, w_codes, w_scales, x_codes, x_scales, name):
     return product
 
 
-def quantise_and_multiply(nc, pool, psum, w_grouped, x_codes, x_scales, name):
-    w_codes, w_scales = quantise(nc, pool, w_grouped, name)
-    return multiply(nc, psum, w_codes, w_scales, x_codes, x_scales, name)
-
-
-def rotation_terms(nc, pool, product, table, name):
-    pairs = product[:].rearrange("p (c e) -> p c e", e=2)
-    cos_sin = table[:, 1:3, :].rearrange("p e c -> p c e")
-    minus_sin_cos = table[:, 0:2, :].rearrange("p e c -> p c e")
-    from_even = pool.tile([P, PAIRS, 2], F32, name=name + "_from_even")
-    from_odd = pool.tile([P, PAIRS, 2], F32, name=name + "_from_odd")
-    nc.vector.tensor_tensor(
-        out=from_even[:], in0=pairs[:, :, 0:1].to_broadcast([P, PAIRS, 2]), in1=cos_sin, op=ALU.mult
-    )
-    nc.vector.tensor_tensor(
-        out=from_odd[:],
-        in0=pairs[:, :, 1:2].to_broadcast([P, PAIRS, 2]),
-        in1=minus_sin_cos,
-        op=ALU.mult,
-    )
-    return from_even, from_odd
-
-
-def add_and_store(nc, add_engine, terms, out):
-    from_even, from_odd = terms
-    add_engine.tensor_tensor(out=from_even[:], in0=from_even[:], in1=from_odd[:], op=ALU.add)
-    nc.sync.dma_start(
-        out=out.rearrange("b s h d -> (b s) (h d)"), in_=from_even[:].rearrange("p c e -> p (c e)")
-    )
+def multiply_turned(nc, codes, scales, x_codes, x_scales, out_of):
+    for j in range(BLOCKS):
+        features = slice(P * j, P * (j + 1))
+        nc.tensor.matmul_mx(
+            out=out_of(j),
+            lhsT=codes[:, features].bitcast(FP8X4),
+            lhsT_scale=scales[:, features],
+            rhs=x_codes[:].bitcast(FP8X4),
+            rhs_scale=x_scales[:],
+            start=True,
+            stop=True,
+        )
 
 
 def tile_selfattention_s_kernel(tc, x, Wq, Wk, Wv, st_pos, out_0, out_1, out_2):
@@ -165,12 +116,9 @@ def tile_selfattention_s_kernel(tc, x, Wq, Wk, Wv, st_pos, out_0, out_1, out_2):
         unused = pool.tile([P, 1], F32)
         nc.vector.memset(zero[:], 0.0)
         nc.scalar.activation(out=unused[:], in_=zero[:], func=ACT.Sin)
-        quarter_turn = pool.tile([P, 1], F32)
-        nc.vector.tensor_scalar(
-            out=quarter_turn[:], in0=zero[:], scalar1=math.pi / 2.0, scalar2=None, op0=ALU.add
-        )
 
-        x_rows = pool.tile([P, K], BF16)
+        x_rows = pool.tile([P, K], BF16, align_bytes=64)
+        nc.sync.dma_start(out=x_rows[:], in_=x.rearrange("b s k -> (b s) k"))
         rows_of = {}
         grouped_of = {}
         for name, weight in (("q", Wq), ("k", Wk), ("v", Wv)):
@@ -179,59 +127,239 @@ def tile_selfattention_s_kernel(tc, x, Wq, Wk, Wv, st_pos, out_0, out_1, out_2):
             nc.sync.dma_start(
                 out=rows_of[name][:], in_=weight.rearrange("(p t) n -> p t n", t=PACK)
             )
-            if name == "q":
-                nc.sync.dma_start(out=x_rows[:], in_=x.rearrange("b s k -> (b s) k"))
 
-        head_index = pool.tile([P, HEADS, 1], I32)
+        position = pool.tile([P, 1], I32)
+        nc.gpsimd.iota(out=position[:], pattern=[[0, 1]], base=0, channel_multiplier=1)
+        first_head = pool.tile([P, BLOCKS], I32)
         nc.gpsimd.iota(
-            out=head_index[:], pattern=[[1, HEADS], [0, 1]], base=0, channel_multiplier=0
+            out=first_head[:], pattern=[[HEADS // BLOCKS, BLOCKS]], base=0, channel_multiplier=0
         )
         identity = pool.tile([P, P], F32)
         masks.make_identity(nc, identity[:])
-        phase = build_rotation_phases(nc, pool, head_index)
+        diagonal = identity[:].rearrange("p (c e) -> p c e", e=2)
 
-        vector_share = slice(0, VECTOR_COLUMNS)
-        scalar_share = slice(VECTOR_COLUMNS, N)
+        bits = pool.tile([P, 4], I32)
+        for b in range(4):
+            nc.vector.tensor_scalar(
+                out=bits[:, b : b + 1],
+                in0=position[:],
+                scalar1=1 + b,
+                scalar2=1,
+                op0=ALU.logical_shift_right,
+                op1=ALU.bitwise_and,
+            )
+        head_in_block = pool.tile([P, 1], I32)
+        nc.vector.tensor_scalar(
+            out=head_in_block[:],
+            in0=position[:],
+            scalar1=5,
+            scalar2=None,
+            op0=ALU.logical_shift_right,
+        )
+        odd = pool.tile([P, 1], I32)
+        nc.vector.tensor_scalar(
+            out=odd[:], in0=position[:], scalar1=1, scalar2=None, op0=ALU.bitwise_and
+        )
+        factors = pool.tile([P, 4], F32)
+        for b in range(4):
+            unit = 1.0 / (2.0 * math.pi) if b == 0 else 1.0
+            nc.vector.tensor_scalar(
+                out=factors[:, b : b + 1],
+                in0=bits[:, b : b + 1],
+                scalar1=unit * (ROPE_BASE ** (-(2.0**b) / FREQS) - 1.0),
+                scalar2=unit,
+                op0=ALU.mult,
+                op1=ALU.add,
+            )
+        head = pool.tile([P, BLOCKS], F32)
+        nc.vector.tensor_tensor(
+            out=head[:],
+            in0=first_head[:],
+            in1=head_in_block[:].to_broadcast([P, BLOCKS]),
+            op=ALU.add,
+        )
+        high = pool.tile([P, 1], F32)
+        nc.vector.tensor_tensor(
+            out=high[:], in0=factors[:, 2:3], in1=factors[:, 3:4], op=ALU.mult
+        )
+        shift = pool.tile([P, 4], F32)
+        for column, (step, start) in enumerate(((0.25, 0.25), (0.25, 0.0), (0.0, 0.25), (0.5, 0.0))):
+            nc.vector.tensor_scalar(
+                out=shift[:, column : column + 1],
+                in0=odd[:],
+                scalar1=step,
+                scalar2=start,
+                op0=ALU.mult,
+                op1=ALU.add,
+            )
+            if column == 1:
+                low = pool.tile([P, BLOCKS, 1], F32)
+                nc.vector.tensor_scalar(
+                    out=low[:, :, 0],
+                    in0=head[:],
+                    scalar1=factors[:, 0:1],
+                    scalar2=factors[:, 1:2],
+                    op0=ALU.mult,
+                    op1=ALU.mult,
+                )
+        own = pool.tile([P, BLOCKS, 4], F32)
+        nc.vector.scalar_tensor_tensor(
+            out=own[:],
+            in0=low[:].to_broadcast([P, BLOCKS, 4]),
+            scalar=high[:],
+            in1=shift[:].rearrange("p (o e) -> p o e", o=1).to_broadcast([P, BLOCKS, 4]),
+            op0=ALU.mult,
+            op1=ALU.add,
+        )
+        same_pair = pool.tile([P, P // 2, 2], F32)
+        nc.vector.tensor_tensor(
+            out=same_pair[:],
+            in0=diagonal[:, :, 0:1].to_broadcast([P, P // 2, 2]),
+            in1=diagonal[:, :, 1:2].to_broadcast([P, P // 2, 2]),
+            op=ALU.add,
+        )
+        own_whole = pool.tile([P, BLOCKS, 4], F32)
+        round_to_integer(nc, own_whole[:], own[:])
+        swap = pool.tile([P, P], F32)
+        nc.vector.tensor_tensor(
+            out=swap[:],
+            in0=same_pair[:].rearrange("p c e -> p (c e)"),
+            in1=identity[:],
+            op=ALU.subtract,
+        )
+        nc.vector.tensor_tensor(out=own[:], in0=own[:], in1=own_whole[:], op=ALU.subtract)
+        busy_codes = pool.tile([P, P], U32, align_bytes=64)
+        busy_scales = pool.tile([P, P], U8, align_bytes=64)
+        nc.vector.quantize_mx(
+            out=busy_codes[:].bitcast(FP8X4), scales=busy_scales[:], in_=x_rows[:]
+        )
+        busy = psum.tile([P, P], F32)
 
-        regroup(nc.vector.tensor_copy, grouped_of["q"], rows_of["q"], vector_share)
-        regroup(nc.scalar.copy, grouped_of["q"], rows_of["q"], scalar_share)
+        def keep_clock(passes):
+            for i in range(passes):
+                nc.tensor.matmul_mx(
+                    out=busy[:],
+                    lhsT=busy_codes[:].bitcast(FP8X4),
+                    lhsT_scale=busy_scales[:],
+                    rhs=busy_codes[:].bitcast(FP8X4),
+                    rhs_scale=busy_scales[:],
+                    start=True,
+                    stop=True,
+                )
+
+        entries = pool.tile([P, BLOCKS, 4], F32)
+        nc.scalar.activation(out=entries[:], in_=own[:], func=ACT.Sin, scale=2.0 * math.pi)
         x_grouped = group_tokens(nc, pool, psum, x_rows, identity)
-        finish_rotation_phases(nc, phase)
-        q_codes, q_scales = quantise(nc, pool, grouped_of["q"], "q")
+
+        def vector_regroup(name, start, stop):
+            regroup(nc.vector.tensor_copy, grouped_of[name], rows_of[name], slice(start, stop))
+
+        def scalar_regroup(name, start, stop):
+            regroup(nc.scalar.copy, grouped_of[name], rows_of[name], slice(start, stop))
+
+        rotation = pool.tile([P, BLOCKS, P // 2, 2], F32)
+        nc.vector.tensor_tensor(
+            out=rotation[:],
+            in0=same_pair[:]
+            .rearrange("p (o c) e -> p o c e", o=1)
+            .to_broadcast([P, BLOCKS, P // 2, 2]),
+            in1=entries[:, :, 0:2]
+            .rearrange("p j (o e) -> p j o e", o=1)
+            .to_broadcast([P, BLOCKS, P // 2, 2]),
+            op=ALU.mult,
+        )
+        keep_clock(18)
+        vector_regroup("q", 0, VECTOR_COLUMNS)
+        scalar_regroup("q", VECTOR_COLUMNS, N)
         x_codes = pool.tile([P, P], U32, align_bytes=64)
         x_scales = pool.tile([P, P], U8, align_bytes=64)
         nc.vector.quantize_mx(out=x_codes[:].bitcast(FP8X4), scales=x_scales[:], in_=x_grouped[:])
-        q_product = multiply(nc, psum, q_codes, q_scales, x_codes, x_scales, "q")
+        q_codes, q_scales = quantise(nc, pool, grouped_of["q"], "q")
 
-        table = pool.tile([P, 3, PAIRS], F32)
-        nc.scalar.activation(
-            out=table[:, 2, :], in_=phase[:, 0, :], func=ACT.Sin, scale=2.0 * math.pi
+        q_turned = psum.tile([P, BLOCKS, P], F32)
+        multiply_turned(nc, q_codes, q_scales, x_codes, x_scales, lambda j: q_turned[:, j, :])
+
+        keep_clock(10)
+        vector_regroup("k", 0, VECTOR_COLUMNS_OF_WK)
+        scalar_regroup("k", VECTOR_COLUMNS_OF_WK, N)
+        first, middle = VECTOR_FIRST_COLUMNS_OF_WV, VECTOR_COLUMNS_OF_WV
+        last = middle + SCALAR_FIRST_COLUMNS_OF_WV
+        vector_regroup("v", 0, first)
+        scalar_regroup("v", middle, last)
+        k_codes, k_scales = quantise(nc, pool, grouped_of["k"], "k")
+        q_features = pool.tile([P, BLOCKS, P], F32)
+        nc.scalar.copy(out=q_features[:], in_=q_turned[:])
+        vector_regroup("v", first, middle)
+        scalar_regroup("v", last, N)
+
+        q_product = psum.tile([P, N], F32)
+
+        def rotate_q(blocks):
+            for j in blocks:
+                nc.tensor.matmul(
+                    q_product[:, P * j : P * (j + 1)],
+                    lhsT=q_features[:, j, :],
+                    rhs=rotation[:, j, :, :].rearrange("p c e -> p (c e)"),
+                    start=True,
+                    stop=True,
+                )
+
+        k_turned = [psum.tile([P, 2, P], F32, name=f"k_turned_{half}") for half in range(2)]
+        multiply_turned(
+            nc, k_codes, k_scales, x_codes, x_scales, lambda j: k_turned[j // 2][:, j % 2, :]
         )
-        nc.scalar.activation(
-            out=table[:, 0, :], in_=phase[:, 0, :], func=ACT.Sin, scale=-2.0 * math.pi
+        rotate_q(range(BLOCKS))
+        v_codes, v_scales = quantise(nc, pool, grouped_of["v"], "v")
+        v_product = multiply(nc, psum, v_codes, v_scales, x_codes, x_scales, "v")
+
+        k_cos = pool.tile([P, BLOCKS, P], F32)
+        k_sin = pool.tile([P, BLOCKS, P], F32)
+        nc.vector.tensor_tensor(
+            out=k_cos[:, 0:2, :],
+            in0=k_turned[0][:],
+            in1=entries[:, 0:2, 2:3].to_broadcast([P, 2, P]),
+            op=ALU.mult,
         )
-
-        regroup(nc.vector.tensor_copy, grouped_of["k"], rows_of["k"], vector_share)
-        regroup(nc.scalar.copy, grouped_of["k"], rows_of["k"], scalar_share)
-        nc.scalar.activation(
-            out=table[:, 1, :],
-            in_=phase[:, 1, :],
-            func=ACT.Sin,
-            scale=2.0 * math.pi,
-            bias=quarter_turn[:],
+        for j in (2, 3):
+            nc.scalar.activation(
+                out=k_cos[:, j, :],
+                in_=k_turned[1][:, j - 2, :],
+                func=ACT.Copy,
+                scale=entries[:, j, 2:3],
+            )
+            nc.scalar.activation(
+                out=k_sin[:, j, :],
+                in_=k_turned[1][:, j - 2, :],
+                func=ACT.Copy,
+                scale=entries[:, j, 3:4],
+            )
+        nc.vector.tensor_tensor(
+            out=k_sin[:, 0:2, :],
+            in0=k_turned[0][:],
+            in1=entries[:, 0:2, 3:4].to_broadcast([P, 2, P]),
+            op=ALU.mult,
         )
-        regroup(nc.vector.tensor_copy, grouped_of["v"], rows_of["v"], slice(0, VECTOR_COLUMNS_OF_WV))
-        regroup(nc.scalar.copy, grouped_of["v"], rows_of["v"], slice(VECTOR_COLUMNS_OF_WV, N))
+        k_product = [psum.tile([P, 2, P], F32, name=f"k_product_{half}") for half in range(2)]
+        for half in (1, 0):
+            for j in (2 * half, 2 * half + 1):
+                out = k_product[half][:, j - 2 * half, :]
+                nc.tensor.matmul(
+                    out, lhsT=k_cos[:, j, :], rhs=identity[:], is_transpose=True, start=True, stop=False
+                )
+                nc.tensor.matmul(
+                    out, lhsT=k_sin[:, j, :], rhs=swap[:], is_transpose=True, start=False, stop=True
+                )
 
-        k_product = quantise_and_multiply(nc, pool, psum, grouped_of["k"], x_codes, x_scales, "k")
-
-        q_terms = rotation_terms(nc, pool, q_product, table, "q")
-        add_and_store(nc, nc.gpsimd, q_terms, out_0)
-
-        v_product = quantise_and_multiply(nc, pool, psum, grouped_of["v"], x_codes, x_scales, "v")
+        q_result = pool.tile([P, N], F32)
+        nc.scalar.copy(out=q_result[:], in_=q_product[:])
+        nc.sync.dma_start(out=out_0.rearrange("b s h d -> (b s) (h d)"), in_=q_result[:])
         v_result = pool.tile([P, N], F32)
-        nc.scalar.copy(out=v_result[:], in_=v_product[:])
+        nc.vector.tensor_copy(out=v_result[:], in_=v_product[:])
         nc.sync.dma_start(out=out_2.rearrange("b s h d -> (b s) (h d)"), in_=v_result[:])
-
-        k_terms = rotation_terms(nc, pool, k_product, table, "k")
-        add_and_store(nc, nc.vector, k_terms, out_1)
+        k_result = pool.tile([P, 2, 2, P], F32)
+        nc.scalar.copy(out=k_result[:, 1, :, :], in_=k_product[1][:])
+        nc.vector.tensor_copy(out=k_result[:, 0, :, :], in_=k_product[0][:])
+        nc.sync.dma_start(
+            out=out_1.rearrange("b s h d -> (b s) (h d)"),
+            in_=k_result[:].rearrange("p g j n -> p (g j n)"),
+        )

@@ -23,11 +23,10 @@ PAIRS = HEADS * FREQS
 ROPE_BASE = 10000.0
 ROUND_TO_INTEGER = 1.5 * 2.0**23
 
-VECTOR_COLUMNS = 320
+VECTOR_COLUMNS = 344
 VECTOR_COLUMNS_OF_WK = 256
-VECTOR_FIRST_COLUMNS_OF_WV = 64
-VECTOR_COLUMNS_OF_WV = 288
-SCALAR_FIRST_COLUMNS_OF_WV = 96
+VECTOR_COLUMNS_OF_WV = 312
+SCALAR_FIRST_COLUMNS_OF_WV = 72
 
 BLOCKS = N // P
 
@@ -258,16 +257,19 @@ def tile_selfattention_s_kernel(tc, x, Wq, Wk, Wv, st_pos, out_0, out_1, out_2):
             regroup(nc.scalar.copy, grouped_of[name], rows_of[name], slice(start, stop))
 
         rotation = pool.tile([P, BLOCKS, P // 2, 2], F32)
-        nc.vector.tensor_tensor(
-            out=rotation[:],
-            in0=same_pair[:]
-            .rearrange("p (o c) e -> p o c e", o=1)
-            .to_broadcast([P, BLOCKS, P // 2, 2]),
-            in1=entries[:, :, 0:2]
-            .rearrange("p j (o e) -> p j o e", o=1)
-            .to_broadcast([P, BLOCKS, P // 2, 2]),
-            op=ALU.mult,
-        )
+
+        def build_rotation(start, stop):
+            shape = [P, stop - start, P // 2, 2]
+            nc.vector.tensor_tensor(
+                out=rotation[:, start:stop, :, :],
+                in0=same_pair[:].rearrange("p (o c) e -> p o c e", o=1).to_broadcast(shape),
+                in1=entries[:, start:stop, 0:2]
+                .rearrange("p j (o e) -> p j o e", o=1)
+                .to_broadcast(shape),
+                op=ALU.mult,
+            )
+
+        build_rotation(0, 2)
         keep_clock(18)
         vector_regroup("q", 0, VECTOR_COLUMNS)
         scalar_regroup("q", VECTOR_COLUMNS, N)
@@ -282,14 +284,14 @@ def tile_selfattention_s_kernel(tc, x, Wq, Wk, Wv, st_pos, out_0, out_1, out_2):
         keep_clock(10)
         vector_regroup("k", 0, VECTOR_COLUMNS_OF_WK)
         scalar_regroup("k", VECTOR_COLUMNS_OF_WK, N)
-        first, middle = VECTOR_FIRST_COLUMNS_OF_WV, VECTOR_COLUMNS_OF_WV
+        middle = VECTOR_COLUMNS_OF_WV
         last = middle + SCALAR_FIRST_COLUMNS_OF_WV
-        vector_regroup("v", 0, first)
+        build_rotation(2, 4)
         scalar_regroup("v", middle, last)
         k_codes, k_scales = quantise(nc, pool, grouped_of["k"], "k")
         q_features = pool.tile([P, BLOCKS, P], F32)
         nc.scalar.copy(out=q_features[:], in_=q_turned[:])
-        vector_regroup("v", first, middle)
+        vector_regroup("v", 0, middle)
         scalar_regroup("v", last, N)
 
         q_product = psum.tile([P, N], F32)

@@ -23,9 +23,9 @@ PAIRS = HEADS * FREQS
 ROPE_BASE = 10000.0
 ROUND_TO_INTEGER = 1.5 * 2.0**23
 
-VECTOR_COLUMNS = 344
-VECTOR_COLUMNS_OF_WK = 256
-VECTOR_COLUMNS_OF_WV = 312
+VECTOR_COLUMNS = 336
+VECTOR_COLUMNS_OF_WK = 232
+VECTOR_COLUMNS_OF_WV = 288
 SCALAR_FIRST_COLUMNS_OF_WV = 72
 
 BLOCKS = N // P

@@ -23,10 +23,10 @@ PAIRS = HEADS * FREQS
 ROPE_BASE = 10000.0
 ROUND_TO_INTEGER = 1.5 * 2.0**23
 
-VECTOR_COLUMNS = 336
-VECTOR_COLUMNS_OF_WK = 232
-VECTOR_COLUMNS_OF_WV = 288
-SCALAR_FIRST_COLUMNS_OF_WV = 72
+VECTOR_COLUMNS = 320
+VECTOR_COLUMNS_OF_WK = 248
+VECTOR_COLUMNS_OF_WV = 304
+SCALAR_FIRST_COLUMNS_OF_WV = 80
 
 BLOCKS = N // P
 
@@ -117,15 +117,16 @@ def tile_selfattention_s_kernel(tc, x, Wq, Wk, Wv, st_pos, out_0, out_1, out_2):
         nc.scalar.activation(out=unused[:], in_=zero[:], func=ACT.Sin)
 
         x_rows = pool.tile([P, K], BF16, align_bytes=64)
-        nc.sync.dma_start(out=x_rows[:], in_=x.rearrange("b s k -> (b s) k"))
         rows_of = {}
         grouped_of = {}
         for name, weight in (("q", Wq), ("k", Wk), ("v", Wv)):
-            rows_of[name] = pool.tile([P, PACK, N], BF16, name=name + "_rows")
+            rows_of[name] = pool.tile([P, PACK, N], BF16, name=name + "_rows", align_bytes=64)
             grouped_of[name] = pool.tile([P, N, PACK], BF16, name=name + "_grouped", align_bytes=64)
             nc.sync.dma_start(
                 out=rows_of[name][:], in_=weight.rearrange("(p t) n -> p t n", t=PACK)
             )
+            if name == "q":
+                nc.sync.dma_start(out=x_rows[:], in_=x.rearrange("b s k -> (b s) k"))
 
         position = pool.tile([P, 1], I32)
         nc.gpsimd.iota(out=position[:], pattern=[[0, 1]], base=0, channel_multiplier=1)
@@ -229,9 +230,6 @@ def tile_selfattention_s_kernel(tc, x, Wq, Wk, Wv, st_pos, out_0, out_1, out_2):
         nc.vector.tensor_tensor(out=own[:], in0=own[:], in1=own_whole[:], op=ALU.subtract)
         busy_codes = pool.tile([P, P], U32, align_bytes=64)
         busy_scales = pool.tile([P, P], U8, align_bytes=64)
-        nc.vector.quantize_mx(
-            out=busy_codes[:].bitcast(FP8X4), scales=busy_scales[:], in_=x_rows[:]
-        )
         busy = psum.tile([P, P], F32)
 
         def keep_clock(passes):
@@ -248,7 +246,6 @@ def tile_selfattention_s_kernel(tc, x, Wq, Wk, Wv, st_pos, out_0, out_1, out_2):
 
         entries = pool.tile([P, BLOCKS, 4], F32)
         nc.scalar.activation(out=entries[:], in_=own[:], func=ACT.Sin, scale=2.0 * math.pi)
-        x_grouped = group_tokens(nc, pool, psum, x_rows, identity)
 
         def vector_regroup(name, start, stop):
             regroup(nc.vector.tensor_copy, grouped_of[name], rows_of[name], slice(start, stop))
@@ -269,19 +266,23 @@ def tile_selfattention_s_kernel(tc, x, Wq, Wk, Wv, st_pos, out_0, out_1, out_2):
                 op=ALU.mult,
             )
 
-        build_rotation(0, 2)
-        keep_clock(18)
         vector_regroup("q", 0, VECTOR_COLUMNS)
         scalar_regroup("q", VECTOR_COLUMNS, N)
+        nc.vector.quantize_mx(
+            out=busy_codes[:].bitcast(FP8X4), scales=busy_scales[:], in_=rows_of["q"][:, 0, :]
+        )
+        x_grouped = group_tokens(nc, pool, psum, x_rows, identity)
+        keep_clock(7)
+        build_rotation(0, 2)
         x_codes = pool.tile([P, P], U32, align_bytes=64)
         x_scales = pool.tile([P, P], U8, align_bytes=64)
-        nc.vector.quantize_mx(out=x_codes[:].bitcast(FP8X4), scales=x_scales[:], in_=x_grouped[:])
         q_codes, q_scales = quantise(nc, pool, grouped_of["q"], "q")
+        nc.vector.quantize_mx(out=x_codes[:].bitcast(FP8X4), scales=x_scales[:], in_=x_grouped[:])
 
         q_turned = psum.tile([P, BLOCKS, P], F32)
         multiply_turned(nc, q_codes, q_scales, x_codes, x_scales, lambda j: q_turned[:, j, :])
 
-        keep_clock(10)
+        keep_clock(12)
         vector_regroup("k", 0, VECTOR_COLUMNS_OF_WK)
         scalar_regroup("k", VECTOR_COLUMNS_OF_WK, N)
         middle = VECTOR_COLUMNS_OF_WV

@@ -134,6 +134,8 @@ def tile_selfattention_s_kernel(tc, x, Wq, Wk, Wv, st_pos, out_0, out_1, out_2):
         nc.gpsimd.iota(
             out=first_head[:], pattern=[[HEADS // BLOCKS, BLOCKS]], base=0, channel_multiplier=0
         )
+        ones = pool.tile([P, P * PACK], BF16, align_bytes=64)
+        nc.gpsimd.memset(ones[:], 1.0)
         identity = pool.tile([P, P], F32)
         masks.make_identity(nc, identity[:])
         diagonal = identity[:].rearrange("p (c e) -> p c e", e=2)
@@ -182,6 +184,26 @@ def tile_selfattention_s_kernel(tc, x, Wq, Wk, Wv, st_pos, out_0, out_1, out_2):
         nc.vector.tensor_tensor(
             out=high[:], in0=factors[:, 2:3], in1=factors[:, 3:4], op=ALU.mult
         )
+        busy_codes = pool.tile([P, P], U32, align_bytes=64)
+        busy_scales = pool.tile([P, P], U8, align_bytes=64)
+        nc.vector.quantize_mx(
+            out=busy_codes[:].bitcast(FP8X4), scales=busy_scales[:], in_=ones[:]
+        )
+        busy = psum.tile([P, P], F32)
+
+        def keep_clock(passes):
+            for i in range(passes):
+                nc.tensor.matmul_mx(
+                    out=busy[:],
+                    lhsT=busy_codes[:].bitcast(FP8X4),
+                    lhsT_scale=busy_scales[:],
+                    rhs=busy_codes[:].bitcast(FP8X4),
+                    rhs_scale=busy_scales[:],
+                    start=True,
+                    stop=True,
+                )
+
+        keep_clock(12)
         shift = pool.tile([P, 4], F32)
         for column, (step, start) in enumerate(((0.25, 0.25), (0.25, 0.0), (0.0, 0.25), (0.5, 0.0))):
             nc.vector.tensor_scalar(
@@ -228,22 +250,6 @@ def tile_selfattention_s_kernel(tc, x, Wq, Wk, Wv, st_pos, out_0, out_1, out_2):
             op=ALU.subtract,
         )
         nc.vector.tensor_tensor(out=own[:], in0=own[:], in1=own_whole[:], op=ALU.subtract)
-        busy_codes = pool.tile([P, P], U32, align_bytes=64)
-        busy_scales = pool.tile([P, P], U8, align_bytes=64)
-        busy = psum.tile([P, P], F32)
-
-        def keep_clock(passes):
-            for i in range(passes):
-                nc.tensor.matmul_mx(
-                    out=busy[:],
-                    lhsT=busy_codes[:].bitcast(FP8X4),
-                    lhsT_scale=busy_scales[:],
-                    rhs=busy_codes[:].bitcast(FP8X4),
-                    rhs_scale=busy_scales[:],
-                    start=True,
-                    stop=True,
-                )
-
         entries = pool.tile([P, BLOCKS, 4], F32)
         nc.scalar.activation(out=entries[:], in_=own[:], func=ACT.Sin, scale=2.0 * math.pi)
 
@@ -268,11 +274,8 @@ def tile_selfattention_s_kernel(tc, x, Wq, Wk, Wv, st_pos, out_0, out_1, out_2):
 
         vector_regroup("q", 0, VECTOR_COLUMNS)
         scalar_regroup("q", VECTOR_COLUMNS, N)
-        nc.vector.quantize_mx(
-            out=busy_codes[:].bitcast(FP8X4), scales=busy_scales[:], in_=rows_of["q"][:, 0, :]
-        )
         x_grouped = group_tokens(nc, pool, psum, x_rows, identity)
-        keep_clock(7)
+        keep_clock(8)
         build_rotation(0, 2)
         x_codes = pool.tile([P, P], U32, align_bytes=64)
         x_scales = pool.tile([P, P], U8, align_bytes=64)

@@ -135,7 +135,7 @@ def tile_selfattention_s_kernel(tc, x, Wq, Wk, Wv, st_pos, out_0, out_1, out_2):
             out=first_head[:], pattern=[[HEADS // BLOCKS, BLOCKS]], base=0, channel_multiplier=0
         )
         ones = pool.tile([P, P * PACK], BF16, align_bytes=64)
-        nc.gpsimd.memset(ones[:], 1.0)
+        nc.gpsimd.memset(ones[:].bitcast(F32), 1.0)
         identity = pool.tile([P, P], F32)
         masks.make_identity(nc, identity[:])
         diagonal = identity[:].rearrange("p (c e) -> p c e", e=2)

import math

import concourse.masks as masks
import concourse.mybir as mybir

F32 = mybir.dt.float32
BF16 = mybir.dt.bfloat16
I32 = mybir.dt.int32
U32 = mybir.dt.uint32
U8 = mybir.dt.uint8
FP8X4 = mybir.dt.float8_e4m3fn_x4
ALU = mybir.AluOpType
ACT = mybir.ActivationFunctionType

P = 128
PACK = 4
K = P * PACK
N = 512
HEADS = 16
HEAD_DIM = N // HEADS
FREQS = HEAD_DIM // 2
PAIRS = HEADS * FREQS
ROPE_BASE = 10000.0
ROUND_TO_INTEGER = 1.5 * 2.0**23

VECTOR_COLUMNS = 320
VECTOR_COLUMNS_OF_WK = 248
VECTOR_COLUMNS_OF_WV = 304
SCALAR_FIRST_COLUMNS_OF_WV = 80

BLOCKS = N // P

FLOPS = 3 * 2 * P * K * N


def round_to_integer(nc, out, in_):
    nc.vector.tensor_scalar(
        out=out,
        in0=in_,
        scalar1=ROUND_TO_INTEGER,
        scalar2=ROUND_TO_INTEGER,
        op0=ALU.add,
        op1=ALU.subtract,
    )


def group_tokens(nc, pool, psum, x_rows, identity):
    x_words = x_rows[:].bitcast(F32).rearrange("r (p u) -> r u p", u=2)
    x_flipped = psum.tile([P, 2, P], F32, tag="x_flipped")
    for u in range(2):
        nc.tensor.transpose(x_flipped[:, u, :], x_words[:, u, :], identity[:])

    x_grouped = pool.tile([P, P * PACK], BF16, align_bytes=64)
    nc.scalar.copy(
        out=x_grouped[:].bitcast(F32).rearrange("p (r u) -> p r u", u=2),
        in_=x_flipped[:].rearrange("p u r -> p r u"),
    )
    return x_grouped


def regroup(copy, w_grouped, w_rows, columns):
    copy(
        out=w_grouped[:, columns, :].rearrange("p (c i) t -> p c t i", i=4),
        in_=w_rows[:, :, columns].rearrange("p t (c i) -> p c t i", i=4),
    )


def quantise(nc, pool, w_grouped, name):
    w_codes = pool.tile([P, N], U32, name=name + "_codes", align_bytes=64)
    w_scales = pool.tile([P, N], U8, name=name + "_scales", align_bytes=64)
    nc.vector.quantize_mx(
        out=w_codes[:].bitcast(FP8X4),
        scales=w_scales[:],
        in_=w_grouped[:].rearrange("p n t -> p (n t)"),
    )
    return w_codes, w_scales


def multiply(nc, psum, w_codes, w_scales, x_codes, x_scales, name):
    product = psum.tile([P, N], F32, name=name + "_product", tag="x_flipped")
    nc.tensor.matmul_mx(
        out=product[:],
        lhsT=x_codes[:].bitcast(FP8X4),
        lhsT_scale=x_scales[:],
        rhs=w_codes[:].bitcast(FP8X4),
        rhs_scale=w_scales[:],
        start=True,
        stop=True,
    )
    return product


def multiply_turned(nc, codes, scales, x_codes, x_scales, out_of):
    for j in range(BLOCKS):
        features = slice(P * j, P * (j + 1))
        nc.tensor.matmul_mx(
            out=out_of(j),
            lhsT=codes[:, features].bitcast(FP8X4),
            lhsT_scale=scales[:, features],
            rhs=x_codes[:].bitcast(FP8X4),
            rhs_scale=x_scales[:],
            start=True,
            stop=True,
        )


def tile_selfattention_s_kernel(tc, x, Wq, Wk, Wv, st_pos, out_0, out_1, out_2):
    nc = tc.nc
    with (
        tc.tile_pool(name="sbuf", bufs=1) as pool,
        tc.psum_pool(name="psum", bufs=1) as psum,
        tc.manual_schedule(),
    ):
        zero = pool.tile([P, 1], F32)
        unused = pool.tile([P, 1], F32)
        nc.vector.memset(zero[:], 0.0)
        nc.scalar.activation(out=unused[:], in_=zero[:], func=ACT.Sin)

        x_rows = pool.tile([P, K], BF16, align_bytes=64)
        rows_of = {}
        grouped_of = {}
        for name, weight in (("q", Wq), ("k", Wk), ("v", Wv)):
            rows_of[name] = pool.tile([P, PACK, N], BF16, name=name + "_rows", align_bytes=64)
            grouped_of[name] = pool.tile([P, N, PACK], BF16, name=name + "_grouped", align_bytes=64)
            nc.sync.dma_start(
                out=rows_of[name][:], in_=weight.rearrange("(p t) n -> p t n", t=PACK)
            )
            if name == "q":
                nc.sync.dma_start(out=x_rows[:], in_=x.rearrange("b s k -> (b s) k"))

        position = pool.tile([P, 1], I32)
        nc.gpsimd.iota(out=position[:], pattern=[[0, 1]], base=0, channel_multiplier=1)
        first_head = pool.tile([P, BLOCKS], I32)
        nc.gpsimd.iota(
            out=first_head[:], pattern=[[HEADS // BLOCKS, BLOCKS]], base=0, channel_multiplier=0
        )
        ones = pool.tile([P, P * PACK], BF16, align_bytes=64)
        nc.gpsimd.memset(ones[:].bitcast(F32), 1.0)
        identity = pool.tile([P, P], F32)
        masks.make_identity(nc, identity[:])
        diagonal = identity[:].rearrange("p (c e) -> p c e", e=2)

        bits = pool.tile([P, 4], I32)
        for b in range(4):
            nc.vector.tensor_scalar(
                out=bits[:, b : b + 1],
                in0=position[:],
                scalar1=1 + b,
                scalar2=1,
                op0=ALU.logical_shift_right,
                op1=ALU.bitwise_and,
            )
        head_in_block = pool.tile([P, 1], I32)
        nc.vector.tensor_scalar(
            out=head_in_block[:],
            in0=position[:],
            scalar1=5,
            scalar2=None,
            op0=ALU.logical_shift_right,
        )
        odd = pool.tile([P, 1], I32)
        nc.vector.tensor_scalar(
            out=odd[:], in0=position[:], scalar1=1, scalar2=None, op0=ALU.bitwise_and
        )
        factors = pool.tile([P, 4], F32)
        for b in range(4):
            unit = 1.0 / (2.0 * math.pi) if b == 0 else 1.0
            nc.vector.tensor_scalar(
                out=factors[:, b : b + 1],
                in0=bits[:, b : b + 1],
                scalar1=unit * (ROPE_BASE ** (-(2.0**b) / FREQS) - 1.0),
                scalar2=unit,
                op0=ALU.mult,
                op1=ALU.add,
            )
        head = pool.tile([P, BLOCKS], F32)
        nc.vector.tensor_tensor(
            out=head[:],
            in0=first_head[:],
            in1=head_in_block[:].to_broadcast([P, BLOCKS]),
            op=ALU.add,
        )
        high = pool.tile([P, 1], F32)
        nc.vector.tensor_tensor(
            out=high[:], in0=factors[:, 2:3], in1=factors[:, 3:4], op=ALU.mult
        )
        busy_codes = pool.tile([P, P], U32, align_bytes=64)
        busy_scales = pool.tile([P, P], U8, align_bytes=64)
        nc.vector.quantize_mx(
            out=busy_codes[:].bitcast(FP8X4), scales=busy_scales[:], in_=ones[:]
        )
        busy = psum.tile([P, P], F32)

        def keep_clock(passes):
            for i in range(passes):
                nc.tensor.matmul_mx(
                    out=busy[:],
                    lhsT=busy_codes[:].bitcast(FP8X4),
                    lhsT_scale=busy_scales[:],
                    rhs=busy_codes[:].bitcast(FP8X4),
                    rhs_scale=busy_scales[:],
                    start=True,
                    stop=True,
                )

        keep_clock(12)
        shift = pool.tile([P, 4], F32)
        for column, (step, start) in enumerate(((0.25, 0.25), (0.25, 0.0), (0.0, 0.25), (0.5, 0.0))):
            nc.vector.tensor_scalar(
                out=shift[:, column : column + 1],
                in0=odd[:],
                scalar1=step,
                scalar2=start,
                op0=ALU.mult,
                op1=ALU.add,
            )
            if column == 1:
                low = pool.tile([P, BLOCKS, 1], F32)
                nc.vector.tensor_scalar(
                    out=low[:, :, 0],
                    in0=head[:],
                    scalar1=factors[:, 0:1],
                    scalar2=factors[:, 1:2],
                    op0=ALU.mult,
                    op1=ALU.mult,
                )
        own = pool.tile([P, BLOCKS, 4], F32)
        nc.vector.scalar_tensor_tensor(
            out=own[:],
            in0=low[:].to_broadcast([P, BLOCKS, 4]),
            scalar=high[:],
            in1=shift[:].rearrange("p (o e) -> p o e", o=1).to_broadcast([P, BLOCKS, 4]),
            op0=ALU.mult,
            op1=ALU.add,
        )
        same_pair = pool.tile([P, P // 2, 2], F32)
        nc.vector.tensor_tensor(
            out=same_pair[:],
            in0=diagonal[:, :, 0:1].to_broadcast([P, P // 2, 2]),
            in1=diagonal[:, :, 1:2].to_broadcast([P, P // 2, 2]),
            op=ALU.add,
        )
        own_whole = pool.tile([P, BLOCKS, 4], F32)
        round_to_integer(nc, own_whole[:], own[:])
        swap = pool.tile([P, P], F32)
        nc.vector.tensor_tensor(
            out=swap[:],
            in0=same_pair[:].rearrange("p c e -> p (c e)"),
            in1=identity[:],
            op=ALU.subtract,
        )
        nc.vector.tensor_tensor(out=own[:], in0=own[:], in1=own_whole[:], op=ALU.subtract)
        entries = pool.tile([P, BLOCKS, 4], F32)
        nc.scalar.activation(out=entries[:], in_=own[:], func=ACT.Sin, scale=2.0 * math.pi)

        def vector_regroup(name, start, stop):
            regroup(nc.vector.tensor_copy, grouped_of[name], rows_of[name], slice(start, stop))

        def scalar_regroup(name, start, stop):
            regroup(nc.scalar.copy, grouped_of[name], rows_of[name], slice(start, stop))

        rotation = pool.tile([P, BLOCKS, P // 2, 2], F32)

        def build_rotation(start, stop):
            shape = [P, stop - start, P // 2, 2]
            nc.vector.tensor_tensor(
                out=rotation[:, start:stop, :, :],
                in0=same_pair[:].rearrange("p (o c) e -> p o c e", o=1).to_broadcast(shape),
                in1=entries[:, start:stop, 0:2]
                .rearrange("p j (o e) -> p j o e", o=1)
                .to_broadcast(shape),
                op=ALU.mult,
            )

        vector_regroup("q", 0, VECTOR_COLUMNS)
        scalar_regroup("q", VECTOR_COLUMNS, N)
        x_grouped = group_tokens(nc, pool, psum, x_rows, identity)
        keep_clock(8)
        build_rotation(0, 2)
        x_codes = pool.tile([P, P], U32, align_bytes=64)
        x_scales = pool.tile([P, P], U8, align_bytes=64)
        q_codes, q_scales = quantise(nc, pool, grouped_of["q"], "q")
        nc.vector.quantize_mx(out=x_codes[:].bitcast(FP8X4), scales=x_scales[:], in_=x_grouped[:])

        q_turned = psum.tile([P, BLOCKS, P], F32)
        multiply_turned(nc, q_codes, q_scales, x_codes, x_scales, lambda j: q_turned[:, j, :])

        keep_clock(12)
        vector_regroup("k", 0, VECTOR_COLUMNS_OF_WK)
        scalar_regroup("k", VECTOR_COLUMNS_OF_WK, N)
        middle = VECTOR_COLUMNS_OF_WV
        last = middle + SCALAR_FIRST_COLUMNS_OF_WV
        build_rotation(2, 4)
        scalar_regroup("v", middle, last)
        k_codes, k_scales = quantise(nc, pool, grouped_of["k"], "k")
        q_features = pool.tile([P, BLOCKS, P], F32)
        nc.scalar.copy(out=q_features[:], in_=q_turned[:])
        vector_regroup("v", 0, middle)
        scalar_regroup("v", last, N)

        q_product = psum.tile([P, N], F32)

        def rotate_q(blocks):
            for j in blocks:
                nc.tensor.matmul(
                    q_product[:, P * j : P * (j + 1)],
                    lhsT=q_features[:, j, :],
                    rhs=rotation[:, j, :, :].rearrange("p c e -> p (c e)"),
                    start=True,
                    stop=True,
                )

        k_turned = [psum.tile([P, 2, P], F32, name=f"k_turned_{half}") for half in range(2)]
        multiply_turned(
            nc, k_codes, k_scales, x_codes, x_scales, lambda j: k_turned[j // 2][:, j % 2, :]
        )
        rotate_q(range(BLOCKS))
        v_codes, v_scales = quantise(nc, pool, grouped_of["v"], "v")
        v_product = multiply(nc, psum, v_codes, v_scales, x_codes, x_scales, "v")

        k_cos = pool.tile([P, BLOCKS, P], F32)
        k_sin = pool.tile([P, BLOCKS, P], F32)
        nc.vector.tensor_tensor(
            out=k_cos[:, 0:2, :],
            in0=k_turned[0][:],
            in1=entries[:, 0:2, 2:3].to_broadcast([P, 2, P]),
            op=ALU.mult,
        )
        for j in (2, 3):
            nc.scalar.activation(
                out=k_cos[:, j, :],
                in_=k_turned[1][:, j - 2, :],
                func=ACT.Copy,
                scale=entries[:, j, 2:3],
            )
            nc.scalar.activation(
                out=k_sin[:, j, :],
                in_=k_turned[1][:, j - 2, :],
                func=ACT.Copy,
                scale=entries[:, j, 3:4],
            )
        nc.vector.tensor_tensor(
            out=k_sin[:, 0:2, :],
            in0=k_turned[0][:],
            in1=entries[:, 0:2, 3:4].to_broadcast([P, 2, P]),
            op=ALU.mult,
        )
        k_product = [psum.tile([P, 2, P], F32, name=f"k_product_{half}") for half in range(2)]
        for half in (1, 0):
            for j in (2 * half, 2 * half + 1):
                out = k_product[half][:, j - 2 * half, :]
                nc.tensor.matmul(
                    out, lhsT=k_cos[:, j, :], rhs=identity[:], is_transpose=True, start=True, stop=False
                )
                nc.tensor.matmul(
                    out, lhsT=k_sin[:, j, :], rhs=swap[:], is_transpose=True, start=False, stop=True
                )

        q_result = pool.tile([P, N], F32)
        nc.scalar.copy(out=q_result[:], in_=q_product[:])
        nc.sync.dma_start(out=out_0.rearrange("b s h d -> (b s) (h d)"), in_=q_result[:])
        v_result = pool.tile([P, N], F32)
        nc.vector.tensor_copy(out=v_result[:], in_=v_product[:])
        nc.sync.dma_start(out=out_2.rearrange("b s h d -> (b s) (h d)"), in_=v_result[:])
        k_result = pool.tile([P, 2, 2, P], F32)
        nc.scalar.copy(out=k_result[:, 1, :, :], in_=k_product[1][:])
        nc.vector.tensor_copy(out=k_result[:, 0, :, :], in_=k_product[0][:])
        nc.sync.dma_start(
            out=out_1.rearrange("b s h d -> (b s) (h d)"),
            in_=k_result[:].rearrange("p g j n -> p (g j n)"),
        )
